import numpy as np
import ml_dtypes


def mxq(x, axis, fmt="e4m3"):
    dtype, down = {"e4m3": (ml_dtypes.float8_e4m3fn, 7), "e5m2": (ml_dtypes.float8_e5m2, 14)}[fmt]
    v = np.moveaxis(np.asarray(x, np.float32).astype(ml_dtypes.bfloat16).astype(np.float64), axis, -1)
    blocks = v.reshape(v.shape[:-1] + (-1, 32))
    amax = np.abs(blocks).max(-1, keepdims=True)
    byte = np.maximum(np.where(amax > 0, np.frexp(amax)[1] - 1 + 127, 0) - down, 1)
    scale = np.exp2(byte - 127.0)
    codes = (blocks / scale).astype(np.float32).astype(dtype).astype(np.float64)
    return np.moveaxis((codes * scale).reshape(v.shape), -1, axis)


WIDE = False


def mx_kscale(k):
    if not WIDE:
        return np.ones(k)
    levels = np.array([10, -10, 5, -5, 0])
    a = np.random.permutation(np.resize(levels, k // 512 * 4)).reshape(k // 512, 4)
    idx = np.arange(k)
    return np.exp2(a[idx // 512, idx % 128 // 32])


BF16 = ml_dtypes.bfloat16


def bf(x):
    return np.asarray(x, np.float32).astype(BF16)


def f64(x):
    return np.asarray(x).astype(np.float64)


E2M1 = np.array([0.0, 0.5, 1.0, 1.5, 2.0, 3.0, 4.0, 6.0, -0.0, -0.5, -1.0, -1.5, -2.0, -3.0, -4.0, -6.0])


def pack_weight(w, fmt):
    k, n = w.shape
    w = f64(bf(w)).reshape(k // 32, 32, n)
    amax = np.abs(w).max(1)
    if fmt == "e4m3":
        byte = np.frexp(amax)[1] - 1 + 127 - 7
    else:
        mant, ex = np.frexp(amax / 6.0)
        byte = np.where(mant > 0.5, ex, ex - 1) + 127
    byte = np.clip(np.where(amax > 0, byte, 1), 1, 254)
    scaled = (w * np.exp2(127.0 - byte)[:, None, :]).reshape(k, n).astype(np.float32)
    by_word = np.ascontiguousarray(scaled.reshape(k // 512, 128, 4, n).transpose(0, 1, 3, 2))
    if fmt == "e4m3":
        words = by_word.astype(ml_dtypes.float8_e4m3fn).view(np.uint8)
    else:
        c = by_word.astype(ml_dtypes.float4_e2m1fn).view(np.uint8) & 0xF
        words = c[..., 0::2] | (c[..., 1::2] << 4)
    return np.ascontiguousarray(words), np.ascontiguousarray(byte.astype(np.uint8).reshape(k // 512, 16, n))


def unpack_weight(words, scales, fmt):
    g, p, n, _ = words.shape
    if fmt == "e4m3":
        vals = np.ascontiguousarray(words).view(ml_dtypes.float8_e4m3fn).astype(np.float64)
    else:
        nib = np.empty((g, p, n, 4), np.uint8)
        nib[..., 0::2] = words & 0xF
        nib[..., 1::2] = words >> 4
        vals = E2M1[nib]
    vals = vals * np.repeat(np.exp2(scales.astype(np.float64) - 127.0), 8, axis=1)[..., None]
    return vals.transpose(0, 1, 3, 2).reshape(g * 512, n)


B, S, D, E = 4, 2048, 1024, 128
THETA = 10000.0


def rope_tables():
    inv = 1.0 / THETA ** (np.arange(0, E, 2).astype(np.float64) / E)
    ang = np.outer(np.arange(S).astype(np.float64), inv)
    return np.cos(ang), np.sin(ang)


def rotate(u, cos, sin):
    ur, ui = u[..., 0::2], u[..., 1::2]
    return np.stack([ur * cos - ui * sin, ur * sin + ui * cos], axis=-1).reshape(B, S, E)


def setup_inputs():
    s = mx_kscale(D)
    x = bf(np.random.standard_normal((B, S, D)) * s)
    wq_words, wq_scales = pack_weight((np.random.standard_normal((E, D)) / np.sqrt(D) / s).T, "e4m3")
    wk_words, wk_scales = pack_weight((np.random.standard_normal((E, D)) / np.sqrt(D) / s).T, "e4m3")
    return {"x": x,
            "wq_words": wq_words, "wq_scales": wq_scales,
            "wk_words": wk_words, "wk_scales": wk_scales}


def reference(x, wq_words, wq_scales, wk_words, wk_scales):
    xm = mxq(f64(x), 2, "e4m3")
    xq = xm @ unpack_weight(wq_words, wq_scales, "e4m3")
    xk = xm @ unpack_weight(wk_words, wk_scales, "e4m3")
    cos, sin = rope_tables()
    return rotate(xq, cos, sin), rotate(xk, cos, sin)

@@ -1,0 +1,219 @@
+import math
+from contextlib import ExitStack
+
+import concourse.mybir as mybir
+from concourse.masks import make_identity
+
+BF16 = mybir.dt.bfloat16
+F32 = mybir.dt.float32
+I32 = mybir.dt.int32
+U32 = mybir.dt.uint32
+U8 = mybir.dt.uint8
+FP8X4 = mybir.dt.float8_e4m3fn_x4
+ALU = mybir.AluOpType
+SIN = mybir.ActivationFunctionType.Sin
+
+B, S, D, E = 4, 2048, 1024, 128
+THETA = 10000.0
+FLOPS = 2 * B * S * D * 2 * E
+
+P = 128
+PACK = 4
+K_PASS = P * PACK
+PASSES = D // K_PASS
+WORDS = 2
+PAIRS = E // 2
+TILES = 2
+HALVES = 2
+ROWS = HALVES * TILES
+ROUND_TOKENS = ROWS * P
+ROUNDS = B * S // ROUND_TOKENS
+QUARTERS = S // ROUND_TOKENS
+AHEAD = 4
+ROUND_MAGIC = 1.5 * 2.0**23
+COARSE = 8
+FINE = PAIRS // COARSE
+
+
+def tile_attention_pa_t_kernel(tc, x, wq_words, wq_scales, wk_words, wk_scales, out_0, out_1):
+    nc = tc.nc
+    x_rows = x.flatten_outer_dims()
+    out_rows = [out_0.flatten_outer_dims(), out_1.flatten_outer_dims()]
+
+    with ExitStack() as ctx:
+        ctx.enter_context(tc.manual_schedule())
+        const = ctx.enter_context(tc.tile_pool(name="const", bufs=1))
+        x_pool = ctx.enter_context(tc.tile_pool(name="x_pool", bufs=HALVES * (AHEAD + 2)))
+        grouped_pool = ctx.enter_context(tc.tile_pool(name="grouped_pool", bufs=2 * HALVES))
+        mx_pool = ctx.enter_context(tc.tile_pool(name="mx_pool", bufs=2 * HALVES))
+        term_pool = ctx.enter_context(tc.tile_pool(name="term_pool", bufs=2 * HALVES))
+        res_pool = ctx.enter_context(tc.tile_pool(name="res_pool", bufs=3))
+        psum_t = ctx.enter_context(tc.psum_pool(name="psum_t", bufs=ROWS))
+        psum_u = ctx.enter_context(tc.psum_pool(name="psum_u", bufs=2 * HALVES))
+
+        def load_round(n):
+            rows = x_rows[n * ROUND_TOKENS : (n + 1) * ROUND_TOKENS, :].rearrange("(p j) d -> p j d", j=ROWS)
+            halves = []
+            for h in range(HALVES):
+                x_half = x_pool.tile([P, TILES, D], BF16, name="x_half")
+                nc.sync.dma_start(out=x_half[:], in_=rows[:, h * TILES : (h + 1) * TILES, :])
+                halves.append(x_half)
+            return halves
+
+        loaded = {}
+        loaded[0] = load_round(0)
+        loaded[1] = load_round(1)
+
+        w_codes = const.tile([P, PASSES, 2, E], U32, align_bytes=64)
+        w_scales = const.tile([P, PASSES, 2, E], U8, align_bytes=64)
+        nc.vector.memset(w_scales[:].bitcast(I32), 0)
+        for w, (words, scales) in enumerate(((wq_words, wq_scales), (wk_words, wk_scales))):
+            nc.sync.dma_start(
+                out=w_codes[:, :, w, :].bitcast(I32),
+                in_=words.rearrange("g p n t -> p g (n t)").bitcast(I32),
+            )
+            by_quadrant = scales.rearrange("g (q r) n -> q r g n", r=4)
+            for q in range(4):
+                nc.sync.dma_start(
+                    out=w_scales[32 * q : 32 * q + 4, :, w, :].bitcast(I32),
+                    in_=by_quadrant[q].bitcast(I32),
+                )
+        for n in range(2, AHEAD):
+            loaded[n] = load_round(n)
+
+        ident = const.tile([P, P], F32)
+        make_identity(nc, ident[:])
+
+        ones = const.tile([P, 1], F32)
+        nc.vector.memset(ones[:], 1.0)
+        warm = const.tile([P, 1], F32)
+        nc.scalar.activation(out=warm[:], in_=ones[:], func=SIN)
+        coarse = const.tile([P, COARSE], F32)
+        fine = const.tile([P, FINE], F32)
+        for a in range(COARSE):
+            factor = THETA ** (-a * FINE / PAIRS) / (2.0 * math.pi)
+            nc.vector.tensor_scalar(out=coarse[:, a : a + 1], in0=ones[:], scalar1=factor, scalar2=None, op0=ALU.mult)
+        for b in range(FINE):
+            factor = THETA ** (-b / PAIRS)
+            nc.vector.tensor_scalar(out=fine[:, b : b + 1], in0=ones[:], scalar1=factor, scalar2=None, op0=ALU.mult)
+        turns = const.tile([P, COARSE, FINE], F32)
+        nc.vector.tensor_tensor(
+            out=turns[:],
+            in0=coarse[:].unsqueeze(2).to_broadcast([P, COARSE, FINE]),
+            in1=fine[:].unsqueeze(1).to_broadcast([P, COARSE, FINE]),
+            op=ALU.mult,
+        )
+        position_int = const.tile([P, QUARTERS * ROWS], I32)
+        nc.gpsimd.iota(position_int[:], pattern=[[ROUND_TOKENS, QUARTERS], [1, ROWS]], base=0, channel_multiplier=ROWS)
+        position = const.tile([P, QUARTERS * ROWS], F32)
+        nc.vector.tensor_copy(out=position[:], in_=position_int[:])
+
+        parts = []
+        for c in range(QUARTERS):
+            phase = const.tile([P, 2, ROWS, PAIRS], F32, name="phase%d" % c)
+            nc.vector.tensor_tensor(
+                out=phase[:, 1],
+                in0=position[:, c * ROWS : (c + 1) * ROWS].unsqueeze(2).to_broadcast([P, ROWS, PAIRS]),
+                in1=turns[:].rearrange("p a b -> p (a b)").unsqueeze(1).to_broadcast([P, ROWS, PAIRS]),
+                op=ALU.mult,
+            )
+            nc.vector.tensor_scalar(out=phase[:, 0], in0=phase[:, 1], scalar1=0.25, scalar2=None, op0=ALU.add)
+            whole = const.tile([P, 2, ROWS, PAIRS], F32, name="whole%d" % c)
+            nc.vector.tensor_scalar(
+                out=whole[:], in0=phase[:], scalar1=ROUND_MAGIC, scalar2=ROUND_MAGIC, op0=ALU.add, op1=ALU.subtract
+            )
+            part = const.tile([P, 3, ROWS, PAIRS], F32, name="part%d" % c)
+            nc.gpsimd.tensor_tensor(out=part[:, 1:3], in0=phase[:], in1=whole[:], op=ALU.subtract)
+            nc.gpsimd.tensor_scalar(out=part[:, 0], in0=part[:, 2], scalar1=-1.0, scalar2=0.0, op0=ALU.mult, op1=ALU.add)
+            parts.append(part)
+
+        for_even = const.tile([P, QUARTERS * ROWS, E], F32)
+        for_odd = const.tile([P, QUARTERS * ROWS, E], F32)
+
+        def sines(c):
+            for table, first in ((for_even, 1), (for_odd, 0)):
+                nc.scalar.activation(
+                    out=table[:, c * ROWS : (c + 1) * ROWS, :].rearrange("p j (i m) -> p j i m", m=2),
+                    in_=parts[c][:, first : first + 2].rearrange("p m j i -> p j i m"),
+                    func=SIN,
+                    scale=2.0 * math.pi,
+                )
+
+        def transpose_half(x_half):
+            x_words = x_half[:].bitcast(F32)
+            grouped = grouped_pool.tile([P, TILES, PASSES, P, PACK], BF16, align_bytes=64)
+            for s in range(TILES):
+                flipped = psum_t.tile([P, PASSES, WORDS, P], F32)
+                for g in range(PASSES):
+                    for u in range(WORDS):
+                        first = g * P * WORDS + u
+                        nc.tensor.transpose(
+                            flipped[:, g, u, :], x_words[:, s, first : (g + 1) * P * WORDS : WORDS], ident[:]
+                        )
+                nc.scalar.copy(out=grouped[:, s].bitcast(F32), in_=flipped[:].rearrange("p g u t -> p g t u"))
+            return grouped
+
+        def quantise_half(grouped):
+            x_codes = mx_pool.tile([P, TILES, PASSES, P], U32, align_bytes=64)
+            x_scales = mx_pool.tile([P, TILES, PASSES, P], U8, align_bytes=64)
+            nc.vector.quantize_mx(
+                out=x_codes[:].rearrange("p s g t -> p (s g t)").bitcast(FP8X4),
+                scales=x_scales[:].rearrange("p s g t -> p (s g t)"),
+                in_=grouped[:].rearrange("p s g t c -> p (s g t c)"),
+            )
+            return x_codes, x_scales
+
+        def project_half(x_codes, x_scales):
+            product = psum_u.tile([P, TILES, 2 * E], F32)
+            for s in range(TILES):
+                for g in range(PASSES):
+                    nc.tensor.matmul_mx(
+                        out=product[:, s, :],
+                        lhsT=x_codes[:, s, g, :].bitcast(FP8X4),
+                        lhsT_scale=x_scales[:, s, g, :],
+                        rhs=w_codes[:, g].rearrange("p w n -> p (w n)").bitcast(FP8X4),
+                        rhs_scale=w_scales[:, g].rearrange("p w n -> p (w n)"),
+                        start=(g == 0),
+                        stop=(g == PASSES - 1),
+                    )
+            return product
+
+        def rotate_half(n, h, product, rotated):
+            shape = [P, TILES, 2, PAIRS, 2]
+            first = (n % QUARTERS) * ROWS + h * TILES
+            members = product[:].rearrange("p s (w i m) -> p s w i m", w=2, m=2)
+            from_even = term_pool.tile(shape, F32)
+            from_odd = term_pool.tile(shape, F32)
+            for term, m, table in ((from_even, 0, for_even), (from_odd, 1, for_odd)):
+                factors = table[:, first : first + TILES, :].rearrange("p s (i m) -> p s i m", m=2)
+                nc.vector.tensor_tensor(
+                    out=term[:],
+                    in0=members[:, :, :, :, m : m + 1].to_broadcast(shape),
+                    in1=factors.unsqueeze(2).to_broadcast(shape),
+                    op=ALU.mult,
+                )
+            nc.gpsimd.tensor_tensor(
+                out=rotated[:, :, h * TILES : (h + 1) * TILES, :].rearrange("p w s e -> p s w e"),
+                in0=from_even[:].rearrange("p s w i m -> p s w (i m)"),
+                in1=from_odd[:].rearrange("p s w i m -> p s w (i m)"),
+                op=ALU.add,
+            )
+
+        quantised = []
+        for n in range(ROUNDS + 1):
+            previous = quantised
+            if n + AHEAD < ROUNDS:
+                loaded[n + AHEAD] = load_round(n + AHEAD)
+            if n < ROUNDS:
+                grouped_halves = [transpose_half(x_half) for x_half in loaded[n]]
+                if n < QUARTERS:
+                    sines(n)
+                quantised = [quantise_half(grouped) for grouped in grouped_halves]
+            if n >= 1:
+                products = [project_half(x_codes, x_scales) for x_codes, x_scales in previous]
+                rotated = res_pool.tile([P, 2, ROWS, E], F32)
+                for h in range(HALVES):
+                    rotate_half(n - 1, h, products[h], rotated)
+                for w in range(2):
+                    rows = out_rows[w][(n - 1) * ROUND_TOKENS : n * ROUND_TOKENS, :]
+                    nc.sync.dma_start(out=rows.rearrange("(p j) e -> p j e", j=ROWS), in_=rotated[:, w])

@@ -29,7 +29,10 @@ ROWS = HALVES * TILES
 ROUND_TOKENS = ROWS * P
 ROUNDS = B * S // ROUND_TOKENS
 QUARTERS = S // ROUND_TOKENS
-AHEAD = 4
+UNITS = ROUNDS * HALVES
+AHEAD = 8
+LAG = 2
+EARLY = 4
 ROUND_MAGIC = 1.5 * 2.0**23
 COARSE = 8
 FINE = PAIRS // COARSE
@@ -43,7 +46,7 @@ def tile_attention_pa_t_kernel(tc, x, wq_words, wq_scales, wk_words, wk_scales, 
     with ExitStack() as ctx:
         ctx.enter_context(tc.manual_schedule())
         const = ctx.enter_context(tc.tile_pool(name="const", bufs=1))
-        x_pool = ctx.enter_context(tc.tile_pool(name="x_pool", bufs=HALVES * (AHEAD + 2)))
+        x_pool = ctx.enter_context(tc.tile_pool(name="x_pool", bufs=AHEAD + 4))
         grouped_pool = ctx.enter_context(tc.tile_pool(name="grouped_pool", bufs=2 * HALVES))
         mx_pool = ctx.enter_context(tc.tile_pool(name="mx_pool", bufs=2 * HALVES))
         term_pool = ctx.enter_context(tc.tile_pool(name="term_pool", bufs=2 * HALVES))
@@ -51,18 +54,16 @@ def tile_attention_pa_t_kernel(tc, x, wq_words, wq_scales, wk_words, wk_scales, 
         psum_t = ctx.enter_context(tc.psum_pool(name="psum_t", bufs=ROWS))
         psum_u = ctx.enter_context(tc.psum_pool(name="psum_u", bufs=2 * HALVES))
 
-        def load_round(n):
+        def load_half(m):
+            n, h = divmod(m, HALVES)
             rows = x_rows[n * ROUND_TOKENS : (n + 1) * ROUND_TOKENS, :].rearrange("(p j) d -> p j d", j=ROWS)
-            halves = []
-            for h in range(HALVES):
-                x_half = x_pool.tile([P, TILES, D], BF16, name="x_half")
-                nc.sync.dma_start(out=x_half[:], in_=rows[:, h * TILES : (h + 1) * TILES, :])
-                halves.append(x_half)
-            return halves
+            x_half = x_pool.tile([P, TILES, D], BF16)
+            nc.sync.dma_start(out=x_half[:], in_=rows[:, h * TILES : (h + 1) * TILES, :])
+            return x_half
 
         loaded = {}
-        loaded[0] = load_round(0)
-        loaded[1] = load_round(1)
+        for m in range(EARLY):
+            loaded[m] = load_half(m)
 
         w_codes = const.tile([P, PASSES, 2, E], U32, align_bytes=64)
         w_scales = const.tile([P, PASSES, 2, E], U8, align_bytes=64)
@@ -78,8 +79,8 @@ def tile_attention_pa_t_kernel(tc, x, wq_words, wq_scales, wk_words, wk_scales, 
                     out=w_scales[32 * q : 32 * q + 4, :, w, :].bitcast(I32),
                     in_=by_quadrant[q].bitcast(I32),
                 )
-        for n in range(2, AHEAD):
-            loaded[n] = load_round(n)
+        for m in range(EARLY, AHEAD):
+            loaded[m] = load_half(m)
 
         ident = const.tile([P, P], F32)
         make_identity(nc, ident[:])
@@ -199,21 +200,24 @@ def tile_attention_pa_t_kernel(tc, x, wq_words, wq_scales, wk_words, wk_scales, 
                 op=ALU.add,
             )
 
-        quantised = []
-        for n in range(ROUNDS + 1):
-            previous = quantised
-            if n + AHEAD < ROUNDS:
-                loaded[n + AHEAD] = load_round(n + AHEAD)
-            if n < ROUNDS:
-                grouped_halves = [transpose_half(x_half) for x_half in loaded[n]]
-                if n < QUARTERS:
-                    sines(n)
-                quantised = [quantise_half(grouped) for grouped in grouped_halves]
-            if n >= 1:
-                products = [project_half(x_codes, x_scales) for x_codes, x_scales in previous]
-                rotated = res_pool.tile([P, 2, ROWS, E], F32)
-                for h in range(HALVES):
-                    rotate_half(n - 1, h, products[h], rotated)
-                for w in range(2):
-                    rows = out_rows[w][(n - 1) * ROUND_TOKENS : n * ROUND_TOKENS, :]
-                    nc.sync.dma_start(out=rows.rearrange("(p j) e -> p j e", j=ROWS), in_=rotated[:, w])
+        quantised = {}
+        rotated = None
+        for m in range(UNITS + LAG):
+            if m + AHEAD < UNITS:
+                loaded[m + AHEAD] = load_half(m + AHEAD)
+            if m < UNITS:
+                grouped = transpose_half(loaded[m])
+                if m % HALVES == 0 and m // HALVES < QUARTERS:
+                    sines(m // HALVES)
+                quantised[m] = quantise_half(grouped)
+            if m >= LAG:
+                n, h = divmod(m - LAG, HALVES)
+                x_codes, x_scales = quantised[m - LAG]
+                product = project_half(x_codes, x_scales)
+                if h == 0:
+                    rotated = res_pool.tile([P, 2, ROWS, E], F32, name="rotated")
+                rotate_half(n, h, product, rotated)
+                if h == HALVES - 1:
+                    for w in range(2):
+                        rows = out_rows[w][n * ROUND_TOKENS : (n + 1) * ROUND_TOKENS, :]
+                        nc.sync.dma_start(out=rows.rearrange("(p j) e -> p j e", j=ROWS), in_=rotated[:, w])

@@ -33,6 +33,7 @@ UNITS = ROUNDS * HALVES
 AHEAD = 8
 LAG = 2
 EARLY = 4
+SINES_AFTER = (1, 2, 4, 6)
 ROUND_MAGIC = 1.5 * 2.0**23
 COARSE = 8
 FINE = PAIRS // COARSE
@@ -109,24 +110,36 @@ def tile_attention_pa_t_kernel(tc, x, wq_words, wq_scales, wk_words, wk_scales, 
         position = const.tile([P, QUARTERS * ROWS], F32)
         nc.vector.tensor_copy(out=position[:], in_=position_int[:])
 
-        parts = []
-        for c in range(QUARTERS):
-            phase = const.tile([P, 2, ROWS, PAIRS], F32, name="phase%d" % c)
-            nc.vector.tensor_tensor(
-                out=phase[:, 1],
-                in0=position[:, c * ROWS : (c + 1) * ROWS].unsqueeze(2).to_broadcast([P, ROWS, PAIRS]),
-                in1=turns[:].rearrange("p a b -> p (a b)").unsqueeze(1).to_broadcast([P, ROWS, PAIRS]),
-                op=ALU.mult,
-            )
-            nc.vector.tensor_scalar(out=phase[:, 0], in0=phase[:, 1], scalar1=0.25, scalar2=None, op0=ALU.add)
-            whole = const.tile([P, 2, ROWS, PAIRS], F32, name="whole%d" % c)
-            nc.vector.tensor_scalar(
-                out=whole[:], in0=phase[:], scalar1=ROUND_MAGIC, scalar2=ROUND_MAGIC, op0=ALU.add, op1=ALU.subtract
-            )
-            part = const.tile([P, 3, ROWS, PAIRS], F32, name="part%d" % c)
-            nc.gpsimd.tensor_tensor(out=part[:, 1:3], in0=phase[:], in1=whole[:], op=ALU.subtract)
-            nc.gpsimd.tensor_scalar(out=part[:, 0], in0=part[:, 2], scalar1=-1.0, scalar2=0.0, op0=ALU.mult, op1=ALU.add)
-            parts.append(part)
+        phases = [const.tile([P, 2, ROWS, PAIRS], F32, name="phase%d" % c) for c in range(QUARTERS)]
+        wholes = [const.tile([P, 2, ROWS, PAIRS], F32, name="whole%d" % c) for c in range(QUARTERS)]
+        parts = [const.tile([P, 3, ROWS, PAIRS], F32, name="part%d" % c) for c in range(QUARTERS)]
+
+        def angle_step(step, c):
+            phase, whole, part = phases[c], wholes[c], parts[c]
+            if step == 0:
+                nc.vector.tensor_tensor(
+                    out=phase[:, 1],
+                    in0=position[:, c * ROWS : (c + 1) * ROWS].unsqueeze(2).to_broadcast([P, ROWS, PAIRS]),
+                    in1=turns[:].rearrange("p a b -> p (a b)").unsqueeze(1).to_broadcast([P, ROWS, PAIRS]),
+                    op=ALU.mult,
+                )
+            elif step == 1:
+                nc.vector.tensor_scalar(out=phase[:, 0], in0=phase[:, 1], scalar1=0.25, scalar2=None, op0=ALU.add)
+            elif step == 2:
+                nc.vector.tensor_scalar(
+                    out=whole[:], in0=phase[:], scalar1=ROUND_MAGIC, scalar2=ROUND_MAGIC, op0=ALU.add, op1=ALU.subtract
+                )
+            elif step == 3:
+                nc.vector.tensor_tensor(out=part[:, 1:3], in0=phase[:], in1=whole[:], op=ALU.subtract)
+            else:
+                nc.vector.tensor_scalar(out=part[:, 0], in0=part[:, 2], scalar1=-1.0, scalar2=None, op0=ALU.mult)
+
+        def angle_steps(steps, quarters):
+            for step in steps:
+                for c in quarters:
+                    angle_step(step, c)
+
+        angle_steps(range(5), (0, 1))
 
         for_even = const.tile([P, QUARTERS * ROWS, E], F32)
         for_odd = const.tile([P, QUARTERS * ROWS, E], F32)
@@ -193,7 +206,8 @@ def tile_attention_pa_t_kernel(tc, x, wq_words, wq_scales, wk_words, wk_scales, 
                     in1=factors.unsqueeze(2).to_broadcast(shape),
                     op=ALU.mult,
                 )
-            nc.gpsimd.tensor_tensor(
+            adder = nc.vector if (n == ROUNDS - 1 and h == HALVES - 1) else nc.gpsimd
+            adder.tensor_tensor(
                 out=rotated[:, :, h * TILES : (h + 1) * TILES, :].rearrange("p w s e -> p s w e"),
                 in0=from_even[:].rearrange("p s w i m -> p s w (i m)"),
                 in1=from_odd[:].rearrange("p s w i m -> p s w (i m)"),
@@ -207,9 +221,13 @@ def tile_attention_pa_t_kernel(tc, x, wq_words, wq_scales, wk_words, wk_scales, 
                 loaded[m + AHEAD] = load_half(m + AHEAD)
             if m < UNITS:
                 grouped = transpose_half(loaded[m])
-                if m % HALVES == 0 and m // HALVES < QUARTERS:
-                    sines(m // HALVES)
+                if m in SINES_AFTER:
+                    sines(SINES_AFTER.index(m))
                 quantised[m] = quantise_half(grouped)
+                if m == 0:
+                    angle_steps(range(3), (2, 3))
+                if m == 1:
+                    angle_steps(range(3, 5), (2, 3))
             if m >= LAG:
                 n, h = divmod(m - LAG, HALVES)
                 x_codes, x_scales = quantised[m - LAG]

@@ -31,7 +31,6 @@ ROUNDS = B * S // ROUND_TOKENS
 QUARTERS = S // ROUND_TOKENS
 UNITS = ROUNDS * HALVES
 AHEAD = 8
-LAG = 2
 EARLY = 4
 SINES_AFTER = (1, 2, 4, 6)
 ROUND_MAGIC = 1.5 * 2.0**23
@@ -48,9 +47,9 @@ def tile_attention_pa_t_kernel(tc, x, wq_words, wq_scales, wk_words, wk_scales, 
         ctx.enter_context(tc.manual_schedule())
         const = ctx.enter_context(tc.tile_pool(name="const", bufs=1))
         x_pool = ctx.enter_context(tc.tile_pool(name="x_pool", bufs=AHEAD + 4))
-        grouped_pool = ctx.enter_context(tc.tile_pool(name="grouped_pool", bufs=2 * HALVES))
-        mx_pool = ctx.enter_context(tc.tile_pool(name="mx_pool", bufs=2 * HALVES))
-        term_pool = ctx.enter_context(tc.tile_pool(name="term_pool", bufs=2 * HALVES))
+        grouped_pool = ctx.enter_context(tc.tile_pool(name="grouped_pool", bufs=3))
+        mx_pool = ctx.enter_context(tc.tile_pool(name="mx_pool", bufs=3))
+        term_pool = ctx.enter_context(tc.tile_pool(name="term_pool", bufs=3))
         res_pool = ctx.enter_context(tc.tile_pool(name="res_pool", bufs=3))
         psum_t = ctx.enter_context(tc.psum_pool(name="psum_t", bufs=ROWS))
         psum_u = ctx.enter_context(tc.psum_pool(name="psum_u", bufs=2 * HALVES))
@@ -153,9 +152,8 @@ def tile_attention_pa_t_kernel(tc, x, wq_words, wq_scales, wk_words, wk_scales, 
                     scale=2.0 * math.pi,
                 )
 
-        def transpose_half(x_half):
+        def transpose_half(x_half, grouped, h):
             x_words = x_half[:].bitcast(F32)
-            grouped = grouped_pool.tile([P, TILES, PASSES, P, PACK], BF16, align_bytes=64)
             for s in range(TILES):
                 flipped = psum_t.tile([P, PASSES, WORDS, P], F32)
                 for g in range(PASSES):
@@ -164,12 +162,13 @@ def tile_attention_pa_t_kernel(tc, x, wq_words, wq_scales, wk_words, wk_scales, 
                         nc.tensor.transpose(
                             flipped[:, g, u, :], x_words[:, s, first : (g + 1) * P * WORDS : WORDS], ident[:]
                         )
-                nc.scalar.copy(out=grouped[:, s].bitcast(F32), in_=flipped[:].rearrange("p g u t -> p g t u"))
-            return grouped
+                nc.scalar.copy(
+                    out=grouped[:, h * TILES + s].bitcast(F32), in_=flipped[:].rearrange("p g u t -> p g t u")
+                )
 
-        def quantise_half(grouped):
-            x_codes = mx_pool.tile([P, TILES, PASSES, P], U32, align_bytes=64)
-            x_scales = mx_pool.tile([P, TILES, PASSES, P], U8, align_bytes=64)
+        def quantise_round(grouped):
+            x_codes = mx_pool.tile([P, ROWS, PASSES, P], U32, align_bytes=64)
+            x_scales = mx_pool.tile([P, ROWS, PASSES, P], U8, align_bytes=64)
             nc.vector.quantize_mx(
                 out=x_codes[:].rearrange("p s g t -> p (s g t)").bitcast(FP8X4),
                 scales=x_scales[:].rearrange("p s g t -> p (s g t)"),
@@ -177,14 +176,14 @@ def tile_attention_pa_t_kernel(tc, x, wq_words, wq_scales, wk_words, wk_scales, 
             )
             return x_codes, x_scales
 
-        def project_half(x_codes, x_scales):
+        def project_half(x_codes, x_scales, h):
             product = psum_u.tile([P, TILES, 2 * E], F32)
             for s in range(TILES):
                 for g in range(PASSES):
                     nc.tensor.matmul_mx(
                         out=product[:, s, :],
-                        lhsT=x_codes[:, s, g, :].bitcast(FP8X4),
-                        lhsT_scale=x_scales[:, s, g, :],
+                        lhsT=x_codes[:, h * TILES + s, g, :].bitcast(FP8X4),
+                        lhsT_scale=x_scales[:, h * TILES + s, g, :],
                         rhs=w_codes[:, g].rearrange("p w n -> p (w n)").bitcast(FP8X4),
                         rhs_scale=w_scales[:, g].rearrange("p w n -> p (w n)"),
                         start=(g == 0),
@@ -192,50 +191,69 @@ def tile_attention_pa_t_kernel(tc, x, wq_words, wq_scales, wk_words, wk_scales, 
                     )
             return product
 
-        def rotate_half(n, h, product, rotated):
+        def multiply_half(n, h, product, terms):
             shape = [P, TILES, 2, PAIRS, 2]
             first = (n % QUARTERS) * ROWS + h * TILES
             members = product[:].rearrange("p s (w i m) -> p s w i m", w=2, m=2)
-            from_even = term_pool.tile(shape, F32)
-            from_odd = term_pool.tile(shape, F32)
-            for term, m, table in ((from_even, 0, for_even), (from_odd, 1, for_odd)):
+            for term, m, table in ((terms[0], 0, for_even), (terms[1], 1, for_odd)):
                 factors = table[:, first : first + TILES, :].rearrange("p s (i m) -> p s i m", m=2)
                 nc.vector.tensor_tensor(
-                    out=term[:],
+                    out=term[:, h * TILES : (h + 1) * TILES],
                     in0=members[:, :, :, :, m : m + 1].to_broadcast(shape),
                     in1=factors.unsqueeze(2).to_broadcast(shape),
                     op=ALU.mult,
                 )
-            adder = nc.vector if (n == ROUNDS - 1 and h == HALVES - 1) else nc.gpsimd
-            adder.tensor_tensor(
-                out=rotated[:, :, h * TILES : (h + 1) * TILES, :].rearrange("p w s e -> p s w e"),
-                in0=from_even[:].rearrange("p s w i m -> p s w (i m)"),
-                in1=from_odd[:].rearrange("p s w i m -> p s w (i m)"),
+
+        def store_round(n, w, rotated):
+            rows = out_rows[w][n * ROUND_TOKENS : (n + 1) * ROUND_TOKENS, :]
+            nc.sync.dma_start(out=rows.rearrange("(p j) e -> p j e", j=ROWS), in_=rotated[:, w])
+
+        def add_round(n, terms):
+            rotated = res_pool.tile([P, 2, ROWS, E], F32, name="rotated")
+            nc.gpsimd.tensor_tensor(
+                out=rotated[:].rearrange("p w s e -> p s w e"),
+                in0=terms[0][:].rearrange("p s w i m -> p s w (i m)"),
+                in1=terms[1][:].rearrange("p s w i m -> p s w (i m)"),
                 op=ALU.add,
             )
+            for w in range(2):
+                store_round(n, w, rotated)
+
+        def add_last_round(n, terms):
+            rotated = res_pool.tile([P, 2, ROWS, E], F32, name="rotated")
+            for w in range(2):
+                nc.vector.tensor_tensor(
+                    out=rotated[:, w],
+                    in0=terms[0][:, :, w].rearrange("p s i m -> p s (i m)"),
+                    in1=terms[1][:, :, w].rearrange("p s i m -> p s (i m)"),
+                    op=ALU.add,
+                )
+                store_round(n, w, rotated)
 
         quantised = {}
-        rotated = None
-        for m in range(UNITS + LAG):
-            if m + AHEAD < UNITS:
-                loaded[m + AHEAD] = load_half(m + AHEAD)
-            if m < UNITS:
-                grouped = transpose_half(loaded[m])
-                if m in SINES_AFTER:
-                    sines(SINES_AFTER.index(m))
-                quantised[m] = quantise_half(grouped)
-                if m == 0:
-                    angle_steps(range(3), (2, 3))
-                if m == 1:
-                    angle_steps(range(3, 5), (2, 3))
-            if m >= LAG:
-                n, h = divmod(m - LAG, HALVES)
-                x_codes, x_scales = quantised[m - LAG]
-                product = project_half(x_codes, x_scales)
-                if h == 0:
-                    rotated = res_pool.tile([P, 2, ROWS, E], F32, name="rotated")
-                rotate_half(n, h, product, rotated)
-                if h == HALVES - 1:
-                    for w in range(2):
-                        rows = out_rows[w][n * ROUND_TOKENS : (n + 1) * ROUND_TOKENS, :]
-                        nc.sync.dma_start(out=rows.rearrange("(p j) e -> p j e", j=ROWS), in_=rotated[:, w])
+        for n in range(ROUNDS + 1):
+            if n < ROUNDS:
+                grouped = grouped_pool.tile([P, ROWS, PASSES, P, PACK], BF16, name="grouped", align_bytes=64)
+                for h in range(HALVES):
+                    m = n * HALVES + h
+                    if m + AHEAD < UNITS:
+                        loaded[m + AHEAD] = load_half(m + AHEAD)
+                    transpose_half(loaded[m], grouped, h)
+                    if m in SINES_AFTER:
+                        sines(SINES_AFTER.index(m))
+            if n >= 1:
+                x_codes, x_scales = quantised[n - 1]
+                products = [project_half(x_codes, x_scales, h) for h in range(HALVES)]
+            if n < ROUNDS:
+                quantised[n] = quantise_round(grouped)
+            if n == 0:
+                angle_steps(range(5), (2, 3))
+            if n >= 1:
+                from_even = term_pool.tile([P, ROWS, 2, PAIRS, 2], F32, name="from_even")
+                from_odd = term_pool.tile([P, ROWS, 2, PAIRS, 2], F32, name="from_odd")
+                for h in range(HALVES):
+                    multiply_half(n - 1, h, products[h], (from_even, from_odd))
+                if n < ROUNDS:
+                    add_round(n - 1, (from_even, from_odd))
+                else:
+                    add_last_round(n - 1, (from_even, from_odd))

@@ -32,7 +32,7 @@ QUARTERS = S // ROUND_TOKENS
 UNITS = ROUNDS * HALVES
 AHEAD = 8
 EARLY = 4
-SINES_AFTER = (1, 2, 4, 6)
+SINES_AFTER = (1, 3, 5, 7)
 ROUND_MAGIC = 1.5 * 2.0**23
 COARSE = 8
 FINE = PAIRS // COARSE
@@ -139,6 +139,7 @@ def tile_attention_pa_t_kernel(tc, x, wq_words, wq_scales, wk_words, wk_scales, 
                     angle_step(step, c)
 
         angle_steps(range(5), (0, 1))
+        angle_steps(range(3), (2, 3))
 
         for_even = const.tile([P, QUARTERS * ROWS, E], F32)
         for_odd = const.tile([P, QUARTERS * ROWS, E], F32)
@@ -208,8 +209,7 @@ def tile_attention_pa_t_kernel(tc, x, wq_words, wq_scales, wk_words, wk_scales, 
             rows = out_rows[w][n * ROUND_TOKENS : (n + 1) * ROUND_TOKENS, :]
             nc.sync.dma_start(out=rows.rearrange("(p j) e -> p j e", j=ROWS), in_=rotated[:, w])
 
-        def add_round(n, terms):
-            rotated = res_pool.tile([P, 2, ROWS, E], F32, name="rotated")
+        def add_round(n, terms, rotated):
             nc.gpsimd.tensor_tensor(
                 out=rotated[:].rearrange("p w s e -> p s w e"),
                 in0=terms[0][:].rearrange("p s w i m -> p s w (i m)"),
@@ -231,6 +231,7 @@ def tile_attention_pa_t_kernel(tc, x, wq_words, wq_scales, wk_words, wk_scales, 
                 store_round(n, w, rotated)
 
         quantised = {}
+        terms_of = {}
         for n in range(ROUNDS + 1):
             if n < ROUNDS:
                 grouped = grouped_pool.tile([P, ROWS, PASSES, P, PACK], BF16, name="grouped", align_bytes=64)
@@ -244,16 +245,21 @@ def tile_attention_pa_t_kernel(tc, x, wq_words, wq_scales, wk_words, wk_scales, 
             if n >= 1:
                 x_codes, x_scales = quantised[n - 1]
                 products = [project_half(x_codes, x_scales, h) for h in range(HALVES)]
+            if n >= 2:
+                rotated = res_pool.tile([P, 2, ROWS, E], F32, name="rotated")
             if n < ROUNDS:
+                if n >= 2:
+                    last_words = grouped[:, ROWS - 1, PASSES - 1, P - 1, :].bitcast(F32)
+                    nc.vector.tensor_copy(out=rotated[:, 0, 0, 0:1], in_=last_words[:, 1:2])
                 quantised[n] = quantise_round(grouped)
             if n == 0:
-                angle_steps(range(5), (2, 3))
+                angle_steps(range(3, 5), (2, 3))
+            if n >= 2:
+                add_round(n - 2, terms_of[n - 2], rotated)
             if n >= 1:
                 from_even = term_pool.tile([P, ROWS, 2, PAIRS, 2], F32, name="from_even")
                 from_odd = term_pool.tile([P, ROWS, 2, PAIRS, 2], F32, name="from_odd")
+                terms_of[n - 1] = (from_even, from_odd)
                 for h in range(HALVES):
-                    multiply_half(n - 1, h, products[h], (from_even, from_odd))
-                if n < ROUNDS:
-                    add_round(n - 1, (from_even, from_odd))
-                else:
-                    add_last_round(n - 1, (from_even, from_odd))
+                    multiply_half(n - 1, h, products[h], terms_of[n - 1])
+        add_last_round(ROUNDS - 1, terms_of[ROUNDS - 1])

@@ -199,7 +199,7 @@ def tile_attention_pa_t_kernel(tc, x, wq_words, wq_scales, wk_words, wk_scales, 
             for term, m, table in ((terms[0], 0, for_even), (terms[1], 1, for_odd)):
                 factors = table[:, first : first + TILES, :].rearrange("p s (i m) -> p s i m", m=2)
                 nc.vector.tensor_tensor(
-                    out=term[:, h * TILES : (h + 1) * TILES],
+                    out=term[:, :, h * TILES : (h + 1) * TILES].rearrange("p w s i m -> p s w i m"),
                     in0=members[:, :, :, :, m : m + 1].to_broadcast(shape),
                     in1=factors.unsqueeze(2).to_broadcast(shape),
                     op=ALU.mult,
@@ -211,9 +211,9 @@ def tile_attention_pa_t_kernel(tc, x, wq_words, wq_scales, wk_words, wk_scales, 
 
         def add_round(n, terms, rotated):
             nc.gpsimd.tensor_tensor(
-                out=rotated[:].rearrange("p w s e -> p s w e"),
-                in0=terms[0][:].rearrange("p s w i m -> p s w (i m)"),
-                in1=terms[1][:].rearrange("p s w i m -> p s w (i m)"),
+                out=rotated[:].rearrange("p w s e -> p (w s e)"),
+                in0=terms[0][:].rearrange("p w s i m -> p (w s i m)"),
+                in1=terms[1][:].rearrange("p w s i m -> p (w s i m)"),
                 op=ALU.add,
             )
             for w in range(2):
@@ -223,9 +223,9 @@ def tile_attention_pa_t_kernel(tc, x, wq_words, wq_scales, wk_words, wk_scales, 
             rotated = res_pool.tile([P, 2, ROWS, E], F32, name="rotated")
             for w in range(2):
                 nc.vector.tensor_tensor(
-                    out=rotated[:, w],
-                    in0=terms[0][:, :, w].rearrange("p s i m -> p s (i m)"),
-                    in1=terms[1][:, :, w].rearrange("p s i m -> p s (i m)"),
+                    out=rotated[:, w].rearrange("p s e -> p (s e)"),
+                    in0=terms[0][:, w].rearrange("p s i m -> p (s i m)"),
+                    in1=terms[1][:, w].rearrange("p s i m -> p (s i m)"),
                     op=ALU.add,
                 )
                 store_round(n, w, rotated)
@@ -257,8 +257,8 @@ def tile_attention_pa_t_kernel(tc, x, wq_words, wq_scales, wk_words, wk_scales, 
             if n >= 2:
                 add_round(n - 2, terms_of[n - 2], rotated)
             if n >= 1:
-                from_even = term_pool.tile([P, ROWS, 2, PAIRS, 2], F32, name="from_even")
-                from_odd = term_pool.tile([P, ROWS, 2, PAIRS, 2], F32, name="from_odd")
+                from_even = term_pool.tile([P, 2, ROWS, PAIRS, 2], F32, name="from_even")
+                from_odd = term_pool.tile([P, 2, ROWS, PAIRS, 2], F32, name="from_odd")
                 terms_of[n - 1] = (from_even, from_odd)
                 for h in range(HALVES):
                     multiply_half(n - 1, h, products[h], terms_of[n - 1])

@@ -32,7 +32,7 @@ QUARTERS = S // ROUND_TOKENS
 UNITS = ROUNDS * HALVES
 AHEAD = 8
 EARLY = 4
-SINES_AFTER = (1, 3, 5, 7)
+SINES_AFTER = (3, 5, 7, 9)
 ROUND_MAGIC = 1.5 * 2.0**23
 COARSE = 8
 FINE = PAIRS // COARSE

@@ -141,14 +141,13 @@ def tile_attention_pa_t_kernel(tc, x, wq_words, wq_scales, wk_words, wk_scales, 
         angle_steps(range(5), (0, 1))
         angle_steps(range(3), (2, 3))
 
-        for_even = const.tile([P, QUARTERS * ROWS, E], F32)
-        for_odd = const.tile([P, QUARTERS * ROWS, E], F32)
+        factors = const.tile([P, QUARTERS * HALVES, 2, TILES, E], F32)
 
         def sines(c):
-            for table, first in ((for_even, 1), (for_odd, 0)):
+            for k, first in ((0, 1), (1, 0)):
                 nc.scalar.activation(
-                    out=table[:, c * ROWS : (c + 1) * ROWS, :].rearrange("p j (i m) -> p j i m", m=2),
-                    in_=parts[c][:, first : first + 2].rearrange("p m j i -> p j i m"),
+                    out=factors[:, c * HALVES : (c + 1) * HALVES, k].rearrange("p h s (i m) -> p h s i m", m=2),
+                    in_=parts[c][:, first : first + 2].rearrange("p m (h s) i -> p h s i m", h=HALVES),
                     func=SIN,
                     scale=2.0 * math.pi,
                 )
@@ -193,17 +192,15 @@ def tile_attention_pa_t_kernel(tc, x, wq_words, wq_scales, wk_words, wk_scales, 
             return product
 
         def multiply_half(n, h, product, terms):
-            shape = [P, TILES, 2, PAIRS, 2]
-            first = (n % QUARTERS) * ROWS + h * TILES
-            members = product[:].rearrange("p s (w i m) -> p s w i m", w=2, m=2)
-            for term, m, table in ((terms[0], 0, for_even), (terms[1], 1, for_odd)):
-                factors = table[:, first : first + TILES, :].rearrange("p s (i m) -> p s i m", m=2)
-                nc.vector.tensor_tensor(
-                    out=term[:, :, h * TILES : (h + 1) * TILES].rearrange("p w s i m -> p s w i m"),
-                    in0=members[:, :, :, :, m : m + 1].to_broadcast(shape),
-                    in1=factors.unsqueeze(2).to_broadcast(shape),
-                    op=ALU.mult,
-                )
+            shape = [P, 2, TILES, 2, PAIRS, 2]
+            members = product[:].rearrange("p s (w i k) -> p k s w i", w=2, k=2)
+            table = factors[:, (n % QUARTERS) * HALVES + h].rearrange("p k s (i m) -> p k s i m", m=2)
+            nc.vector.tensor_tensor(
+                out=terms[:, h],
+                in0=members.unsqueeze(5).to_broadcast(shape),
+                in1=table.unsqueeze(3).to_broadcast(shape),
+                op=ALU.mult,
+            )
 
         def store_round(n, w, rotated):
             rows = out_rows[w][n * ROUND_TOKENS : (n + 1) * ROUND_TOKENS, :]
@@ -211,9 +208,9 @@ def tile_attention_pa_t_kernel(tc, x, wq_words, wq_scales, wk_words, wk_scales, 
 
         def add_round(n, terms, rotated):
             nc.gpsimd.tensor_tensor(
-                out=rotated[:].rearrange("p w s e -> p (w s e)"),
-                in0=terms[0][:].rearrange("p w s i m -> p (w s i m)"),
-                in1=terms[1][:].rearrange("p w s i m -> p (w s i m)"),
+                out=rotated[:].rearrange("p w (h s) e -> p h s w e", h=HALVES),
+                in0=terms[:, :, 0].rearrange("p h s w i m -> p h s w (i m)"),
+                in1=terms[:, :, 1].rearrange("p h s w i m -> p h s w (i m)"),
                 op=ALU.add,
             )
             for w in range(2):
@@ -223,9 +220,9 @@ def tile_attention_pa_t_kernel(tc, x, wq_words, wq_scales, wk_words, wk_scales, 
             rotated = res_pool.tile([P, 2, ROWS, E], F32, name="rotated")
             for w in range(2):
                 nc.vector.tensor_tensor(
-                    out=rotated[:, w].rearrange("p s e -> p (s e)"),
-                    in0=terms[0][:, w].rearrange("p s i m -> p (s i m)"),
-                    in1=terms[1][:, w].rearrange("p s i m -> p (s i m)"),
+                    out=rotated[:, w].rearrange("p (h s) e -> p h s e", h=HALVES),
+                    in0=terms[:, :, 0, :, w].rearrange("p h s i m -> p h s (i m)"),
+                    in1=terms[:, :, 1, :, w].rearrange("p h s i m -> p h s (i m)"),
                     op=ALU.add,
                 )
                 store_round(n, w, rotated)
@@ -257,9 +254,8 @@ def tile_attention_pa_t_kernel(tc, x, wq_words, wq_scales, wk_words, wk_scales, 
             if n >= 2:
                 add_round(n - 2, terms_of[n - 2], rotated)
             if n >= 1:
-                from_even = term_pool.tile([P, 2, ROWS, PAIRS, 2], F32, name="from_even")
-                from_odd = term_pool.tile([P, 2, ROWS, PAIRS, 2], F32, name="from_odd")
-                terms_of[n - 1] = (from_even, from_odd)
+                terms = term_pool.tile([P, HALVES, 2, TILES, 2, PAIRS, 2], F32, name="terms")
+                terms_of[n - 1] = terms
                 for h in range(HALVES):
                     multiply_half(n - 1, h, products[h], terms_of[n - 1])
         add_last_round(ROUNDS - 1, terms_of[ROUNDS - 1])

@@ -61,24 +61,32 @@ def tile_attention_pa_t_kernel(tc, x, wq_words, wq_scales, wk_words, wk_scales, 
             nc.sync.dma_start(out=x_half[:], in_=rows[:, h * TILES : (h + 1) * TILES, :])
             return x_half
 
-        loaded = {}
-        for m in range(EARLY):
-            loaded[m] = load_half(m)
-
         w_codes = const.tile([P, PASSES, 2, E], U32, align_bytes=64)
         w_scales = const.tile([P, PASSES, 2, E], U8, align_bytes=64)
         nc.vector.memset(w_scales[:].bitcast(I32), 0)
-        for w, (words, scales) in enumerate(((wq_words, wq_scales), (wk_words, wk_scales))):
-            nc.sync.dma_start(
-                out=w_codes[:, :, w, :].bitcast(I32),
-                in_=words.rearrange("g p n t -> p g (n t)").bitcast(I32),
-            )
+
+        def load_scales(w, scales):
             by_quadrant = scales.rearrange("g (q r) n -> q r g n", r=4)
             for q in range(4):
                 nc.sync.dma_start(
                     out=w_scales[32 * q : 32 * q + 4, :, w, :].bitcast(I32),
                     in_=by_quadrant[q].bitcast(I32),
                 )
+
+        def load_codes(w, words):
+            nc.sync.dma_start(
+                out=w_codes[:, :, w, :].bitcast(I32),
+                in_=words.rearrange("g p n t -> p g (n t)").bitcast(I32),
+            )
+
+        loaded = {}
+        loaded[0] = load_half(0)
+        load_scales(0, wq_scales)
+        for m in range(1, EARLY):
+            loaded[m] = load_half(m)
+        load_scales(1, wk_scales)
+        load_codes(0, wq_words)
+        load_codes(1, wk_words)
         for m in range(EARLY, AHEAD):
             loaded[m] = load_half(m)
 

@@ -33,6 +33,7 @@ UNITS = ROUNDS * HALVES
 AHEAD = 8
 EARLY = 4
 SINES_AFTER = (3, 5, 7, 9)
+GPSIMD_SHARE = 960
 ROUND_MAGIC = 1.5 * 2.0**23
 COARSE = 8
 FINE = PAIRS // COARSE
@@ -149,13 +150,14 @@ def tile_attention_pa_t_kernel(tc, x, wq_words, wq_scales, wk_words, wk_scales, 
         angle_steps(range(5), (0, 1))
         angle_steps(range(3), (2, 3))
 
-        factors = const.tile([P, QUARTERS * HALVES, 2, TILES, E], F32)
+        for_even = const.tile([P, QUARTERS * ROWS, E], F32)
+        for_odd = const.tile([P, QUARTERS * ROWS, E], F32)
 
         def sines(c):
-            for k, first in ((0, 1), (1, 0)):
+            for table, first in ((for_even, 1), (for_odd, 0)):
                 nc.scalar.activation(
-                    out=factors[:, c * HALVES : (c + 1) * HALVES, k].rearrange("p h s (i m) -> p h s i m", m=2),
-                    in_=parts[c][:, first : first + 2].rearrange("p m (h s) i -> p h s i m", h=HALVES),
+                    out=table[:, c * ROWS : (c + 1) * ROWS, :].rearrange("p j (i m) -> p j i m", m=2),
+                    in_=parts[c][:, first : first + 2].rearrange("p m j i -> p j i m"),
                     func=SIN,
                     scale=2.0 * math.pi,
                 )
@@ -200,37 +202,49 @@ def tile_attention_pa_t_kernel(tc, x, wq_words, wq_scales, wk_words, wk_scales, 
             return product
 
         def multiply_half(n, h, product, terms):
-            shape = [P, 2, TILES, 2, PAIRS, 2]
-            members = product[:].rearrange("p s (w i k) -> p k s w i", w=2, k=2)
-            table = factors[:, (n % QUARTERS) * HALVES + h].rearrange("p k s (i m) -> p k s i m", m=2)
-            nc.vector.tensor_tensor(
-                out=terms[:, h],
-                in0=members.unsqueeze(5).to_broadcast(shape),
-                in1=table.unsqueeze(3).to_broadcast(shape),
-                op=ALU.mult,
-            )
+            shape = [P, TILES, 2, PAIRS, 2]
+            first = (n % QUARTERS) * ROWS + h * TILES
+            members = product[:].rearrange("p s (w i m) -> p s w i m", w=2, m=2)
+            for term, m, table in ((terms[:, 0], 0, for_even), (terms[:, 1], 1, for_odd)):
+                factors = table[:, first : first + TILES, :].rearrange("p s (i m) -> p s i m", m=2)
+                nc.vector.tensor_tensor(
+                    out=term[:, :, h * TILES : (h + 1) * TILES].rearrange("p w s i m -> p s w i m"),
+                    in0=members[:, :, :, :, m : m + 1].to_broadcast(shape),
+                    in1=factors.unsqueeze(2).to_broadcast(shape),
+                    op=ALU.mult,
+                )
 
         def store_round(n, w, rotated):
             rows = out_rows[w][n * ROUND_TOKENS : (n + 1) * ROUND_TOKENS, :]
             nc.sync.dma_start(out=rows.rearrange("(p j) e -> p j e", j=ROWS), in_=rotated[:, w])
 
         def add_round(n, terms, rotated):
+            flat = terms[:].rearrange("p k w s i m -> p k (w s i m)")
             nc.gpsimd.tensor_tensor(
-                out=rotated[:].rearrange("p w (h s) e -> p h s w e", h=HALVES),
-                in0=terms[:, :, 0].rearrange("p h s w i m -> p h s w (i m)"),
-                in1=terms[:, :, 1].rearrange("p h s w i m -> p h s w (i m)"),
+                out=rotated[:].rearrange("p w s e -> p (w s e)")[:, 0:GPSIMD_SHARE],
+                in0=flat[:, 0, 0:GPSIMD_SHARE],
+                in1=flat[:, 1, 0:GPSIMD_SHARE],
                 op=ALU.add,
             )
             for w in range(2):
                 store_round(n, w, rotated)
 
+        def add_rest(terms, rotated):
+            flat = terms[:].rearrange("p k w s i m -> p k (w s i m)")
+            nc.vector.tensor_reduce(
+                out=rotated[:].rearrange("p w s e -> p (w s e)")[:, GPSIMD_SHARE:],
+                in_=flat[:, :, GPSIMD_SHARE:].rearrange("p k e -> p e k"),
+                axis=mybir.AxisListType.X,
+                op=ALU.add,
+            )
+
         def add_last_round(n, terms):
             rotated = res_pool.tile([P, 2, ROWS, E], F32, name="rotated")
             for w in range(2):
                 nc.vector.tensor_tensor(
-                    out=rotated[:, w].rearrange("p (h s) e -> p h s e", h=HALVES),
-                    in0=terms[:, :, 0, :, w].rearrange("p h s i m -> p h s (i m)"),
-                    in1=terms[:, :, 1, :, w].rearrange("p h s i m -> p h s (i m)"),
+                    out=rotated[:, w].rearrange("p s e -> p (s e)"),
+                    in0=terms[:, 0, w].rearrange("p s i m -> p (s i m)"),
+                    in1=terms[:, 1, w].rearrange("p s i m -> p (s i m)"),
                     op=ALU.add,
                 )
                 store_round(n, w, rotated)
@@ -260,9 +274,10 @@ def tile_attention_pa_t_kernel(tc, x, wq_words, wq_scales, wk_words, wk_scales, 
             if n == 0:
                 angle_steps(range(3, 5), (2, 3))
             if n >= 2:
+                add_rest(terms_of[n - 2], rotated)
                 add_round(n - 2, terms_of[n - 2], rotated)
             if n >= 1:
-                terms = term_pool.tile([P, HALVES, 2, TILES, 2, PAIRS, 2], F32, name="terms")
+                terms = term_pool.tile([P, 2, 2, ROWS, PAIRS, 2], F32, name="terms")
                 terms_of[n - 1] = terms
                 for h in range(HALVES):
                     multiply_half(n - 1, h, products[h], terms_of[n - 1])

@@ -33,7 +33,7 @@ UNITS = ROUNDS * HALVES
 AHEAD = 8
 EARLY = 4
 SINES_AFTER = (3, 5, 7, 9)
-GPSIMD_SHARE = 960
+GPSIMD_SHARE = 992
 ROUND_MAGIC = 1.5 * 2.0**23
 COARSE = 8
 FINE = PAIRS // COARSE

import math
from contextlib import ExitStack

import concourse.mybir as mybir
from concourse.masks import make_identity

BF16 = mybir.dt.bfloat16
F32 = mybir.dt.float32
I32 = mybir.dt.int32
U32 = mybir.dt.uint32
U8 = mybir.dt.uint8
FP8X4 = mybir.dt.float8_e4m3fn_x4
ALU = mybir.AluOpType
SIN = mybir.ActivationFunctionType.Sin

B, S, D, E = 4, 2048, 1024, 128
THETA = 10000.0
FLOPS = 2 * B * S * D * 2 * E

P = 128
PACK = 4
K_PASS = P * PACK
PASSES = D // K_PASS
WORDS = 2
PAIRS = E // 2
TILES = 2
HALVES = 2
ROWS = HALVES * TILES
ROUND_TOKENS = ROWS * P
ROUNDS = B * S // ROUND_TOKENS
QUARTERS = S // ROUND_TOKENS
UNITS = ROUNDS * HALVES
AHEAD = 8
EARLY = 4
SINES_AFTER = (3, 5, 7, 9)
GPSIMD_SHARE = 992
ROUND_MAGIC = 1.5 * 2.0**23
COARSE = 8
FINE = PAIRS // COARSE


def tile_attention_pa_t_kernel(tc, x, wq_words, wq_scales, wk_words, wk_scales, out_0, out_1):
    nc = tc.nc
    x_rows = x.flatten_outer_dims()
    out_rows = [out_0.flatten_outer_dims(), out_1.flatten_outer_dims()]

    with ExitStack() as ctx:
        ctx.enter_context(tc.manual_schedule())
        const = ctx.enter_context(tc.tile_pool(name="const", bufs=1))
        x_pool = ctx.enter_context(tc.tile_pool(name="x_pool", bufs=AHEAD + 4))
        grouped_pool = ctx.enter_context(tc.tile_pool(name="grouped_pool", bufs=3))
        mx_pool = ctx.enter_context(tc.tile_pool(name="mx_pool", bufs=3))
        term_pool = ctx.enter_context(tc.tile_pool(name="term_pool", bufs=3))
        res_pool = ctx.enter_context(tc.tile_pool(name="res_pool", bufs=3))
        psum_t = ctx.enter_context(tc.psum_pool(name="psum_t", bufs=ROWS))
        psum_u = ctx.enter_context(tc.psum_pool(name="psum_u", bufs=2 * HALVES))

        def load_half(m):
            n, h = divmod(m, HALVES)
            rows = x_rows[n * ROUND_TOKENS : (n + 1) * ROUND_TOKENS, :].rearrange("(p j) d -> p j d", j=ROWS)
            x_half = x_pool.tile([P, TILES, D], BF16)
            nc.sync.dma_start(out=x_half[:], in_=rows[:, h * TILES : (h + 1) * TILES, :])
            return x_half

        w_codes = const.tile([P, PASSES, 2, E], U32, align_bytes=64)
        w_scales = const.tile([P, PASSES, 2, E], U8, align_bytes=64)
        nc.vector.memset(w_scales[:].bitcast(I32), 0)

        def load_scales(w, scales):
            by_quadrant = scales.rearrange("g (q r) n -> q r g n", r=4)
            for q in range(4):
                nc.sync.dma_start(
                    out=w_scales[32 * q : 32 * q + 4, :, w, :].bitcast(I32),
                    in_=by_quadrant[q].bitcast(I32),
                )

        def load_codes(w, words):
            nc.sync.dma_start(
                out=w_codes[:, :, w, :].bitcast(I32),
                in_=words.rearrange("g p n t -> p g (n t)").bitcast(I32),
            )

        loaded = {}
        loaded[0] = load_half(0)
        load_scales(0, wq_scales)
        for m in range(1, EARLY):
            loaded[m] = load_half(m)
        load_scales(1, wk_scales)
        load_codes(0, wq_words)
        load_codes(1, wk_words)
        for m in range(EARLY, AHEAD):
            loaded[m] = load_half(m)

        ident = const.tile([P, P], F32)
        make_identity(nc, ident[:])

        ones = const.tile([P, 1], F32)
        nc.vector.memset(ones[:], 1.0)
        warm = const.tile([P, 1], F32)
        nc.scalar.activation(out=warm[:], in_=ones[:], func=SIN)
        coarse = const.tile([P, COARSE], F32)
        fine = const.tile([P, FINE], F32)
        for a in range(COARSE):
            factor = THETA ** (-a * FINE / PAIRS) / (2.0 * math.pi)
            nc.vector.tensor_scalar(out=coarse[:, a : a + 1], in0=ones[:], scalar1=factor, scalar2=None, op0=ALU.mult)
        for b in range(FINE):
            factor = THETA ** (-b / PAIRS)
            nc.vector.tensor_scalar(out=fine[:, b : b + 1], in0=ones[:], scalar1=factor, scalar2=None, op0=ALU.mult)
        turns = const.tile([P, COARSE, FINE], F32)
        nc.vector.tensor_tensor(
            out=turns[:],
            in0=coarse[:].unsqueeze(2).to_broadcast([P, COARSE, FINE]),
            in1=fine[:].unsqueeze(1).to_broadcast([P, COARSE, FINE]),
            op=ALU.mult,
        )
        position_int = const.tile([P, QUARTERS * ROWS], I32)
        nc.gpsimd.iota(position_int[:], pattern=[[ROUND_TOKENS, QUARTERS], [1, ROWS]], base=0, channel_multiplier=ROWS)
        position = const.tile([P, QUARTERS * ROWS], F32)
        nc.vector.tensor_copy(out=position[:], in_=position_int[:])

        phases = [const.tile([P, 2, ROWS, PAIRS], F32, name="phase%d" % c) for c in range(QUARTERS)]
        wholes = [const.tile([P, 2, ROWS, PAIRS], F32, name="whole%d" % c) for c in range(QUARTERS)]
        parts = [const.tile([P, 3, ROWS, PAIRS], F32, name="part%d" % c) for c in range(QUARTERS)]

        def angle_step(step, c):
            phase, whole, part = phases[c], wholes[c], parts[c]
            if step == 0:
                nc.vector.tensor_tensor(
                    out=phase[:, 1],
                    in0=position[:, c * ROWS : (c + 1) * ROWS].unsqueeze(2).to_broadcast([P, ROWS, PAIRS]),
                    in1=turns[:].rearrange("p a b -> p (a b)").unsqueeze(1).to_broadcast([P, ROWS, PAIRS]),
                    op=ALU.mult,
                )
            elif step == 1:
                nc.vector.tensor_scalar(out=phase[:, 0], in0=phase[:, 1], scalar1=0.25, scalar2=None, op0=ALU.add)
            elif step == 2:
                nc.vector.tensor_scalar(
                    out=whole[:], in0=phase[:], scalar1=ROUND_MAGIC, scalar2=ROUND_MAGIC, op0=ALU.add, op1=ALU.subtract
                )
            elif step == 3:
                nc.vector.tensor_tensor(out=part[:, 1:3], in0=phase[:], in1=whole[:], op=ALU.subtract)
            else:
                nc.vector.tensor_scalar(out=part[:, 0], in0=part[:, 2], scalar1=-1.0, scalar2=None, op0=ALU.mult)

        def angle_steps(steps, quarters):
            for step in steps:
                for c in quarters:
                    angle_step(step, c)

        angle_steps(range(5), (0, 1))
        angle_steps(range(3), (2, 3))

        for_even = const.tile([P, QUARTERS * ROWS, E], F32)
        for_odd = const.tile([P, QUARTERS * ROWS, E], F32)

        def sines(c):
            for table, first in ((for_even, 1), (for_odd, 0)):
                nc.scalar.activation(
                    out=table[:, c * ROWS : (c + 1) * ROWS, :].rearrange("p j (i m) -> p j i m", m=2),
                    in_=parts[c][:, first : first + 2].rearrange("p m j i -> p j i m"),
                    func=SIN,
                    scale=2.0 * math.pi,
                )

        def transpose_half(x_half, grouped, h):
            x_words = x_half[:].bitcast(F32)
            for s in range(TILES):
                flipped = psum_t.tile([P, PASSES, WORDS, P], F32)
                for g in range(PASSES):
                    for u in range(WORDS):
                        first = g * P * WORDS + u
                        nc.tensor.transpose(
                            flipped[:, g, u, :], x_words[:, s, first : (g + 1) * P * WORDS : WORDS], ident[:]
                        )
                nc.scalar.copy(
                    out=grouped[:, h * TILES + s].bitcast(F32), in_=flipped[:].rearrange("p g u t -> p g t u")
                )

        def quantise_round(grouped):
            x_codes = mx_pool.tile([P, ROWS, PASSES, P], U32, align_bytes=64)
            x_scales = mx_pool.tile([P, ROWS, PASSES, P], U8, align_bytes=64)
            nc.vector.quantize_mx(
                out=x_codes[:].rearrange("p s g t -> p (s g t)").bitcast(FP8X4),
                scales=x_scales[:].rearrange("p s g t -> p (s g t)"),
                in_=grouped[:].rearrange("p s g t c -> p (s g t c)"),
            )
            return x_codes, x_scales

        def project_half(x_codes, x_scales, h):
            product = psum_u.tile([P, TILES, 2 * E], F32)
            for s in range(TILES):
                for g in range(PASSES):
                    nc.tensor.matmul_mx(
                        out=product[:, s, :],
                        lhsT=x_codes[:, h * TILES + s, g, :].bitcast(FP8X4),
                        lhsT_scale=x_scales[:, h * TILES + s, g, :],
                        rhs=w_codes[:, g].rearrange("p w n -> p (w n)").bitcast(FP8X4),
                        rhs_scale=w_scales[:, g].rearrange("p w n -> p (w n)"),
                        start=(g == 0),
                        stop=(g == PASSES - 1),
                    )
            return product

        def multiply_half(n, h, product, terms):
            shape = [P, TILES, 2, PAIRS, 2]
            first = (n % QUARTERS) * ROWS + h * TILES
            members = product[:].rearrange("p s (w i m) -> p s w i m", w=2, m=2)
            for term, m, table in ((terms[:, 0], 0, for_even), (terms[:, 1], 1, for_odd)):
                factors = table[:, first : first + TILES, :].rearrange("p s (i m) -> p s i m", m=2)
                nc.vector.tensor_tensor(
                    out=term[:, :, h * TILES : (h + 1) * TILES].rearrange("p w s i m -> p s w i m"),
                    in0=members[:, :, :, :, m : m + 1].to_broadcast(shape),
                    in1=factors.unsqueeze(2).to_broadcast(shape),
                    op=ALU.mult,
                )

        def store_round(n, w, rotated):
            rows = out_rows[w][n * ROUND_TOKENS : (n + 1) * ROUND_TOKENS, :]
            nc.sync.dma_start(out=rows.rearrange("(p j) e -> p j e", j=ROWS), in_=rotated[:, w])

        def add_round(n, terms, rotated):
            flat = terms[:].rearrange("p k w s i m -> p k (w s i m)")
            nc.gpsimd.tensor_tensor(
                out=rotated[:].rearrange("p w s e -> p (w s e)")[:, 0:GPSIMD_SHARE],
                in0=flat[:, 0, 0:GPSIMD_SHARE],
                in1=flat[:, 1, 0:GPSIMD_SHARE],
                op=ALU.add,
            )
            for w in range(2):
                store_round(n, w, rotated)

        def add_rest(terms, rotated):
            flat = terms[:].rearrange("p k w s i m -> p k (w s i m)")
            nc.vector.tensor_reduce(
                out=rotated[:].rearrange("p w s e -> p (w s e)")[:, GPSIMD_SHARE:],
                in_=flat[:, :, GPSIMD_SHARE:].rearrange("p k e -> p e k"),
                axis=mybir.AxisListType.X,
                op=ALU.add,
            )

        def add_last_round(n, terms):
            rotated = res_pool.tile([P, 2, ROWS, E], F32, name="rotated")
            for w in range(2):
                nc.vector.tensor_tensor(
                    out=rotated[:, w].rearrange("p s e -> p (s e)"),
                    in0=terms[:, 0, w].rearrange("p s i m -> p (s i m)"),
                    in1=terms[:, 1, w].rearrange("p s i m -> p (s i m)"),
                    op=ALU.add,
                )
                store_round(n, w, rotated)

        quantised = {}
        terms_of = {}
        for n in range(ROUNDS + 1):
            if n < ROUNDS:
                grouped = grouped_pool.tile([P, ROWS, PASSES, P, PACK], BF16, name="grouped", align_bytes=64)
                for h in range(HALVES):
                    m = n * HALVES + h
                    if m + AHEAD < UNITS:
                        loaded[m + AHEAD] = load_half(m + AHEAD)
                    transpose_half(loaded[m], grouped, h)
                    if m in SINES_AFTER:
                        sines(SINES_AFTER.index(m))
            if n >= 1:
                x_codes, x_scales = quantised[n - 1]
                products = [project_half(x_codes, x_scales, h) for h in range(HALVES)]
            if n >= 2:
                rotated = res_pool.tile([P, 2, ROWS, E], F32, name="rotated")
            if n < ROUNDS:
                if n >= 2:
                    last_words = grouped[:, ROWS - 1, PASSES - 1, P - 1, :].bitcast(F32)
                    nc.vector.tensor_copy(out=rotated[:, 0, 0, 0:1], in_=last_words[:, 1:2])
                quantised[n] = quantise_round(grouped)
            if n == 0:
                angle_steps(range(3, 5), (2, 3))
            if n >= 2:
                add_rest(terms_of[n - 2], rotated)
                add_round(n - 2, terms_of[n - 2], rotated)
            if n >= 1:
                terms = term_pool.tile([P, 2, 2, ROWS, PAIRS, 2], F32, name="terms")
                terms_of[n - 1] = terms
                for h in range(HALVES):
                    multiply_half(n - 1, h, products[h], terms_of[n - 1])
        add_last_round(ROUNDS - 1, terms_of[ROUNDS - 1])
